import numpy as np
import ml_dtypes


def mxq(x, axis, fmt="e4m3"):
    dtype, down = {"e4m3": (ml_dtypes.float8_e4m3fn, 7), "e5m2": (ml_dtypes.float8_e5m2, 14)}[fmt]
    v = np.moveaxis(np.asarray(x, np.float32).astype(ml_dtypes.bfloat16).astype(np.float64), axis, -1)
    blocks = v.reshape(v.shape[:-1] + (-1, 32))
    amax = np.abs(blocks).max(-1, keepdims=True)
    byte = np.maximum(np.where(amax > 0, np.frexp(amax)[1] - 1 + 127, 0) - down, 1)
    scale = np.exp2(byte - 127.0)
    codes = (blocks / scale).astype(np.float32).astype(dtype).astype(np.float64)
    return np.moveaxis((codes * scale).reshape(v.shape), -1, axis)


WIDE = False


def mx_kscale(k):
    if not WIDE:
        return np.ones(k)
    levels = np.array([10, -10, 5, -5, 0])
    a = np.random.permutation(np.resize(levels, k // 512 * 4)).reshape(k // 512, 4)
    idx = np.arange(k)
    return np.exp2(a[idx // 512, idx % 128 // 32])


BF16 = ml_dtypes.bfloat16


def bf(x):
    return np.asarray(x, np.float32).astype(BF16)


def f64(x):
    return np.asarray(x).astype(np.float64)


E2M1 = np.array([0.0, 0.5, 1.0, 1.5, 2.0, 3.0, 4.0, 6.0, -0.0, -0.5, -1.0, -1.5, -2.0, -3.0, -4.0, -6.0])


def pack_weight(w, fmt):
    k, n = w.shape
    w = f64(bf(w)).reshape(k // 32, 32, n)
    amax = np.abs(w).max(1)
    if fmt == "e4m3":
        byte = np.frexp(amax)[1] - 1 + 127 - 7
    else:
        mant, ex = np.frexp(amax / 6.0)
        byte = np.where(mant > 0.5, ex, ex - 1) + 127
    byte = np.clip(np.where(amax > 0, byte, 1), 1, 254)
    scaled = (w * np.exp2(127.0 - byte)[:, None, :]).reshape(k, n).astype(np.float32)
    by_word = np.ascontiguousarray(scaled.reshape(k // 512, 128, 4, n).transpose(0, 1, 3, 2))
    if fmt == "e4m3":
        words = by_word.astype(ml_dtypes.float8_e4m3fn).view(np.uint8)
    else:
        c = by_word.astype(ml_dtypes.float4_e2m1fn).view(np.uint8) & 0xF
        words = c[..., 0::2] | (c[..., 1::2] << 4)
    return np.ascontiguousarray(words), np.ascontiguousarray(byte.astype(np.uint8).reshape(k // 512, 16, n))


def unpack_weight(words, scales, fmt):
    g, p, n, _ = words.shape
    if fmt == "e4m3":
        vals = np.ascontiguousarray(words).view(ml_dtypes.float8_e4m3fn).astype(np.float64)
    else:
        nib = np.empty((g, p, n, 4), np.uint8)
        nib[..., 0::2] = words & 0xF
        nib[..., 1::2] = words >> 4
        vals = E2M1[nib]
    vals = vals * np.repeat(np.exp2(scales.astype(np.float64) - 127.0), 8, axis=1)[..., None]
    return vals.transpose(0, 1, 3, 2).reshape(g * 512, n)


B, I, O, SEG = 128, 2048, 2048, 4


def sigmoid(v):
    return 1.0 / (1.0 + np.exp(-v))


def setup_inputs():
    s = mx_kscale(I)
    x = bf(np.random.standard_normal((B, I)) * s)
    context = bf(np.random.standard_normal(O))
    prev_activation = bf(np.random.standard_normal((B, O)))
    weight = bf(np.random.standard_normal((O, I)) * 2.0 / np.sqrt(I) / s)
    bias = bf(np.random.standard_normal(O) * 0.5)
    astrocyte_activation = bf(1.0 + 0.5 * np.random.standard_normal(O))
    stack = np.random.standard_normal((O, I, SEG)) * 0.5 / np.sqrt(I) / s[:, None]
    words, scales = pack_weight(stack.reshape(-1, SEG), "e4m3")
    return {
        "x": x,
        "context": context,
        "prev_activation": prev_activation,
        "weight": weight,
        "bias": bias,
        "astrocyte_activation": astrocyte_activation,
        "dendrite_segments_words": words,
        "dendrite_segments_scales": scales,
    }


def reference(x, context, prev_activation, weight, bias, astrocyte_activation, dendrite_segments_words, dendrite_segments_scales):
    xq = mxq(f64(x), 1, "e4m3")
    astro_mod = sigmoid(f64(astrocyte_activation) * f64(context))
    dq = unpack_weight(dendrite_segments_words, dendrite_segments_scales, "e4m3").reshape(O, I, SEG)
    pre = (xq @ dq.transpose(1, 0, 2).reshape(I, O * SEG)).reshape(B, O, SEG)
    dendritic_out = np.maximum(pre, 0.0).sum(axis=2)
    wg = f64(weight) * astro_mod[:, None]
    out = (xq @ mxq(wg, 1, "e4m3").T) + f64(bias)
    return out + dendritic_out

@@ -1,0 +1,224 @@
+from contextlib import ExitStack
+
+import concourse.mybir as mybir
+from concourse.masks import make_identity
+
+F32 = mybir.dt.float32
+BF16 = mybir.dt.bfloat16
+I32 = mybir.dt.int32
+U32 = mybir.dt.uint32
+U8 = mybir.dt.uint8
+FP8X4 = mybir.dt.float8_e4m3fn_x4
+ALU = mybir.AluOpType
+ACT = mybir.ActivationFunctionType
+
+P = 128
+B = 128
+I = 2048
+O = 2048
+SEG = 4
+PACK = 4
+K_PASS = P * PACK
+PASSES = I // K_PASS
+RUNS = I // K_PASS
+QUADRANT = P // RUNS
+RUN_SHARE = QUADRANT * PACK
+SCALE_ROWS = K_PASS // 32
+O_BLOCKS = O // P
+PAIRS = PACK // 2
+PASS_PAIRS = K_PASS // 2
+
+FLOPS = 2 * B * I * (O * SEG + O)
+BYTES = 2 * (B * I + O * I + 3 * O) + O * I * SEG + O * I * SEG // 32 + 4 * B * O
+
+
+def tile_advancedneuroplasticitylayer_w_e_kernel(
+    tc,
+    x,
+    context,
+    prev_activation,
+    weight,
+    bias,
+    astrocyte_activation,
+    dendrite_segments_words,
+    dendrite_segments_scales,
+    out,
+):
+    nc = tc.nc
+    with ExitStack() as stack:
+        stack.enter_context(
+            nc.allow_non_contiguous_dma(reason="the given bytes lie in runs of 16 and 4 bytes")
+        )
+        const = stack.enter_context(tc.tile_pool(name="const", bufs=1))
+        given = stack.enter_context(tc.tile_pool(name="given", bufs=3))
+        loads = stack.enter_context(tc.tile_pool(name="loads", bufs=3))
+        work = stack.enter_context(tc.tile_pool(name="work", bufs=2))
+        turned = stack.enter_context(tc.psum_pool(name="turned", bufs=2))
+        sums = stack.enter_context(tc.psum_pool(name="sums", bufs=2))
+
+        ident = const.tile([P, P], F32)
+        make_identity(nc, ident[:])
+
+        d_planes = const.tile([P, O * SEG], U8, align_bytes=64)
+        nc.vector.memset(d_planes[:].bitcast(I32), 0)
+
+        x_sb = const.tile([P, I], BF16)
+        nc.scalar.dma_start(out=x_sb[:], in_=x)
+        x_sorted = const.tile([P, I], BF16)
+        nc.vector.tensor_copy(
+            out=x_sorted[:].rearrange("b (c s e) -> b c s e", c=PASSES, s=RUNS),
+            in_=x_sb[:].rearrange("b (s c e) -> b c s e", c=PASSES, s=RUNS),
+        )
+        x_pairs = x_sorted[:].bitcast(F32)
+        x_grouped = const.tile([P, PASSES, B, PACK], BF16, align_bytes=64)
+        for half in range(2):
+            x_ps = turned.tile([P, 2, PAIRS, B], F32, tag="w_ps")
+            for ci in range(2):
+                c = 2 * half + ci
+                for u in range(PAIRS):
+                    nc.tensor.transpose(
+                        x_ps[:, ci, u, :],
+                        x_pairs[:, PASS_PAIRS * c + u : PASS_PAIRS * (c + 1) : PAIRS],
+                        ident[:],
+                    )
+            nc.vector.tensor_copy(
+                out=x_grouped[:, 2 * half : 2 * half + 2].bitcast(F32),
+                in_=x_ps[:].rearrange("p c u b -> p c b u"),
+            )
+        x_words = const.tile([P, PASSES * B], U32, align_bytes=64)
+        x_planes = const.tile([P, PASSES * B], U8, align_bytes=64)
+        nc.vector.quantize_mx(
+            out=x_words[:].bitcast(FP8X4),
+            scales=x_planes[:],
+            in_=x_grouped[:].rearrange("p c b t -> p (c b t)"),
+        )
+
+        vectors = const.tile([P, 2, P], BF16)
+        nc.vector.memset(vectors[:], 0.0)
+        nc.scalar.dma_start(
+            out=vectors[0:O_BLOCKS, 0, :],
+            in_=astrocyte_activation.rearrange("(r c) -> r c", c=P),
+        )
+        nc.scalar.dma_start(
+            out=vectors[0:O_BLOCKS, 1, :], in_=context.rearrange("(r c) -> r c", c=P)
+        )
+        product = const.tile([P, P], F32)
+        nc.vector.tensor_tensor(
+            out=product[:], in0=vectors[:, 0, :], in1=vectors[:, 1, :], op=ALU.mult
+        )
+        gate_rows = const.tile([P, P], F32)
+        nc.scalar.activation(out=gate_rows[:], in_=product[:], func=ACT.Sigmoid)
+        gate_ps = turned.tile([P, P], F32, tag="w_ps")
+        nc.tensor.transpose(gate_ps[:], gate_rows[:], ident[:])
+        gate = const.tile([P, O_BLOCKS], F32)
+        nc.vector.tensor_copy(out=gate[:], in_=gate_ps[:, 0:O_BLOCKS])
+
+        bias_all = const.tile([P, O], BF16)
+        nc.scalar.dma_start(out=bias_all[:], in_=bias.partition_broadcast(P))
+
+        words_by_run = dendrite_segments_words.rearrange(
+            "(o s) p n t -> s p o (n t)", s=RUNS
+        ).bitcast(I32)
+        scales_by_run = dendrite_segments_scales.rearrange(
+            "(o s) q n -> s q o n", s=RUNS
+        ).bitcast(I32)
+        out_sb = const.tile([P, O], F32)
+
+        for ob in range(O_BLOCKS):
+            units = slice(ob * P, (ob + 1) * P)
+            columns = slice(ob * P * SEG, (ob + 1) * P * SEG)
+
+            for s in range(RUNS):
+                nc.sync.dma_start(
+                    out=d_planes[QUADRANT * s : QUADRANT * s + SCALE_ROWS, columns]
+                    .bitcast(I32)
+                    .rearrange("q (o w) -> q o w", w=1),
+                    in_=scales_by_run[s, :, units, :],
+                )
+            d_words = []
+            for c in range(PASSES):
+                d_pass = given.tile([P, P * SEG], U32, align_bytes=64, name="d_pass")
+                for s in range(RUNS):
+                    nc.sync.dma_start(
+                        out=d_pass[QUADRANT * s : QUADRANT * (s + 1), :]
+                        .bitcast(I32)
+                        .rearrange("r (o j) -> r o j", j=SEG),
+                        in_=words_by_run[s, QUADRANT * c : QUADRANT * (c + 1), units, :],
+                    )
+                d_words.append(d_pass)
+            w_raw = loads.tile([P, I], BF16)
+            nc.scalar.dma_start(out=w_raw[:], in_=weight[units, :])
+
+            wg = work.tile([P, I], BF16)
+            nc.vector.tensor_scalar_mul(
+                out=wg[:].rearrange("o (c s e) -> o c s e", c=PASSES, s=RUNS),
+                in0=w_raw[:].rearrange("o (s c e) -> o c s e", c=PASSES, s=RUNS),
+                scalar1=gate[:, ob : ob + 1],
+            )
+            w_grouped = work.tile([P, PASSES, P, PACK], BF16, align_bytes=64)
+            for half in range(2):
+                w_ps = turned.tile([P, 2, PAIRS, P], F32, tag="w_ps")
+                for ci in range(2):
+                    c = 2 * half + ci
+                    for u in range(PAIRS):
+                        nc.tensor.transpose(
+                            w_ps[:, ci, u, :],
+                            wg[:].bitcast(F32)[
+                                :, PASS_PAIRS * c + u : PASS_PAIRS * (c + 1) : PAIRS
+                            ],
+                            ident[:],
+                        )
+                nc.scalar.copy(
+                    out=w_grouped[:, 2 * half : 2 * half + 2].bitcast(F32),
+                    in_=w_ps[:].rearrange("p c u o -> p c o u"),
+                )
+            w_words = work.tile([P, PASSES * P], U32, align_bytes=64)
+            w_planes = work.tile([P, PASSES * P], U8, align_bytes=64)
+            nc.vector.quantize_mx(
+                out=w_words[:].bitcast(FP8X4),
+                scales=w_planes[:],
+                in_=w_grouped[:].rearrange("p c o t -> p (c o t)"),
+            )
+
+            lin = sums.tile([P, P], F32)
+            for c in range(PASSES):
+                rows = slice(c * B, (c + 1) * B)
+                nc.tensor.matmul_mx(
+                    out=lin[:],
+                    lhsT=x_words[:, rows].bitcast(FP8X4),
+                    lhsT_scale=x_planes[:, rows],
+                    rhs=w_words[:, c * P : (c + 1) * P].bitcast(FP8X4),
+                    rhs_scale=w_planes[:, c * P : (c + 1) * P],
+                    start=(c == 0),
+                    stop=(c == PASSES - 1),
+                )
+            pre = sums.tile([P, P * SEG], F32)
+            for c in range(PASSES):
+                rows = slice(c * B, (c + 1) * B)
+                nc.tensor.matmul_mx(
+                    out=pre[:],
+                    lhsT=x_words[:, rows].bitcast(FP8X4),
+                    lhsT_scale=x_planes[:, rows],
+                    rhs=d_words[c][:].bitcast(FP8X4),
+                    rhs_scale=d_planes[4 * c : P, columns],
+                    start=(c == 0),
+                    stop=(c == PASSES - 1),
+                )
+
+            lin_bias = work.tile([P, P], F32)
+            nc.vector.tensor_tensor(out=lin_bias[:], in0=lin[:], in1=bias_all[:, units], op=ALU.add)
+            relu = work.tile([P, P * SEG], F32)
+            nc.scalar.activation(out=relu[:], in_=pre[:], func=ACT.Relu)
+            dendritic = work.tile([P, P], F32)
+            nc.vector.tensor_reduce(
+                out=dendritic[:],
+                in_=relu[:].rearrange("p (o j) -> p o j", j=SEG),
+                axis=mybir.AxisListType.X,
+                op=ALU.add,
+            )
+            nc.vector.tensor_tensor(
+                out=out_sb[:, units], in0=lin_bias[:], in1=dendritic[:], op=ALU.add
+            )
+            if ob % 4 == 3:
+                done = slice((ob - 3) * P, (ob + 1) * P)
+                nc.scalar.dma_start(out=out[:, done], in_=out_sb[:, done])

@@ -25,6 +25,7 @@ QUADRANT = P // RUNS
 RUN_SHARE = QUADRANT * PACK
 SCALE_ROWS = K_PASS // 32
 O_BLOCKS = O // P
+BLOCK_WORDS = 8
 PAIRS = PACK // 2
 PASS_PAIRS = K_PASS // 2
 
@@ -58,9 +59,6 @@ def tile_advancedneuroplasticitylayer_w_e_kernel(
 
         ident = const.tile([P, P], F32)
         make_identity(nc, ident[:])
-
-        d_planes = const.tile([P, O * SEG], U8, align_bytes=64)
-        nc.vector.memset(d_planes[:].bitcast(I32), 0)
 
         x_sb = const.tile([P, I], BF16)
         nc.scalar.dma_start(out=x_sb[:], in_=x)
@@ -122,33 +120,27 @@ def tile_advancedneuroplasticitylayer_w_e_kernel(
         scales_by_run = dendrite_segments_scales.rearrange(
             "(o s) q n -> s q o n", s=RUNS
         ).bitcast(I32)
+        d_planes = const.tile([P, O * SEG], U8, align_bytes=64)
         out_sb = const.tile([P, O], F32)
 
         for ob in range(O_BLOCKS):
             units = slice(ob * P, (ob + 1) * P)
             columns = slice(ob * P * SEG, (ob + 1) * P * SEG)
 
+            s_landed = given.tile([P, P, BLOCK_WORDS], I32)
+            nc.vector.memset(s_landed[:], 0)
             for s in range(RUNS):
                 nc.sync.dma_start(
-                    out=d_planes[QUADRANT * s : QUADRANT * s + SCALE_ROWS, columns]
-                    .bitcast(I32)
-                    .rearrange("q (o w) -> q o w", w=1),
+                    out=s_landed[QUADRANT * s : QUADRANT * s + SCALE_ROWS, :, 0:1],
                     in_=scales_by_run[s, :, units, :],
                 )
-            d_words = []
-            for c in range(PASSES):
-                d_pass = given.tile([P, P * SEG], U32, align_bytes=64, name="d_pass")
-                for s in range(RUNS):
-                    nc.sync.dma_start(
-                        out=d_pass[QUADRANT * s : QUADRANT * (s + 1), :]
-                        .bitcast(I32)
-                        .rearrange("r (o j) -> r o j", j=SEG),
-                        in_=words_by_run[s, QUADRANT * c : QUADRANT * (c + 1), units, :],
-                    )
-                d_words.append(d_pass)
+            nc.vector.tensor_copy(
+                out=d_planes[:, columns].bitcast(I32).rearrange("q (o w) -> q o w", w=1),
+                in_=s_landed[:, :, 0:1],
+            )
+
             w_raw = loads.tile([P, I], BF16)
             nc.scalar.dma_start(out=w_raw[:], in_=weight[units, :])
-
             wg = work.tile([P, I], BF16)
             nc.vector.tensor_scalar_mul(
                 out=wg[:].rearrange("o (c s e) -> o c s e", c=PASSES, s=RUNS),
@@ -179,7 +171,6 @@ def tile_advancedneuroplasticitylayer_w_e_kernel(
                 scales=w_planes[:],
                 in_=w_grouped[:].rearrange("p c o t -> p (c o t)"),
             )
-
             lin = sums.tile([P, P], F32)
             for c in range(PASSES):
                 rows = slice(c * B, (c + 1) * B)
@@ -192,21 +183,33 @@ def tile_advancedneuroplasticitylayer_w_e_kernel(
                     start=(c == 0),
                     stop=(c == PASSES - 1),
                 )
+            lin_bias = work.tile([P, P], F32)
+            nc.vector.tensor_tensor(out=lin_bias[:], in0=lin[:], in1=bias_all[:, units], op=ALU.add)
+
             pre = sums.tile([P, P * SEG], F32)
             for c in range(PASSES):
+                d_landed = given.tile([P, P, BLOCK_WORDS], I32)
+                for s in range(RUNS):
+                    nc.sync.dma_start(
+                        out=d_landed[QUADRANT * s : QUADRANT * (s + 1), :, 0:SEG],
+                        in_=words_by_run[s, QUADRANT * c : QUADRANT * (c + 1), units, :],
+                    )
+                d_words = work.tile([P, P * SEG], U32, align_bytes=64)
+                nc.vector.tensor_copy(
+                    out=d_words[:].bitcast(I32).rearrange("r (o j) -> r o j", j=SEG),
+                    in_=d_landed[:, :, 0:SEG],
+                )
                 rows = slice(c * B, (c + 1) * B)
                 nc.tensor.matmul_mx(
                     out=pre[:],
                     lhsT=x_words[:, rows].bitcast(FP8X4),
                     lhsT_scale=x_planes[:, rows],
-                    rhs=d_words[c][:].bitcast(FP8X4),
+                    rhs=d_words[:].bitcast(FP8X4),
                     rhs_scale=d_planes[4 * c : P, columns],
                     start=(c == 0),
                     stop=(c == PASSES - 1),
                 )
 
-            lin_bias = work.tile([P, P], F32)
-            nc.vector.tensor_tensor(out=lin_bias[:], in0=lin[:], in1=bias_all[:, units], op=ALU.add)
             relu = work.tile([P, P * SEG], F32)
             nc.scalar.activation(out=relu[:], in_=pre[:], func=ACT.Relu)
             dendritic = work.tile([P, P], F32)

@@ -25,7 +25,6 @@ QUADRANT = P // RUNS
 RUN_SHARE = QUADRANT * PACK
 SCALE_ROWS = K_PASS // 32
 O_BLOCKS = O // P
-BLOCK_WORDS = 8
 PAIRS = PACK // 2
 PASS_PAIRS = K_PASS // 2
 
@@ -114,30 +113,31 @@ def tile_advancedneuroplasticitylayer_w_e_kernel(
         bias_all = const.tile([P, O], BF16)
         nc.scalar.dma_start(out=bias_all[:], in_=bias.partition_broadcast(P))
 
-        words_by_run = dendrite_segments_words.rearrange(
-            "(o s) p n t -> s p o (n t)", s=RUNS
-        ).bitcast(I32)
-        scales_by_run = dendrite_segments_scales.rearrange(
-            "(o s) q n -> s q o n", s=RUNS
-        ).bitcast(I32)
+        words_by_run = dendrite_segments_words.rearrange("(o s) p n t -> s p o (n t)", s=RUNS)
+        scales_by_run = dendrite_segments_scales.rearrange("(o s) q n -> s q o n", s=RUNS)
+
+        def load_given(s, sbuf_bytes, hbm_bytes, run_words):
+            queue, word = (nc.sync, I32) if s % 2 == 0 else (nc.scalar, F32)
+            queue.dma_start(
+                out=sbuf_bytes.bitcast(word).rearrange("r (o w) -> r o w", w=run_words),
+                in_=hbm_bytes.bitcast(word),
+            )
+
         d_planes = const.tile([P, O * SEG], U8, align_bytes=64)
+        nc.vector.memset(d_planes[:].bitcast(I32), 0)
         out_sb = const.tile([P, O], F32)
 
         for ob in range(O_BLOCKS):
             units = slice(ob * P, (ob + 1) * P)
             columns = slice(ob * P * SEG, (ob + 1) * P * SEG)
 
-            s_landed = given.tile([P, P, BLOCK_WORDS], I32)
-            nc.vector.memset(s_landed[:], 0)
             for s in range(RUNS):
-                nc.sync.dma_start(
-                    out=s_landed[QUADRANT * s : QUADRANT * s + SCALE_ROWS, :, 0:1],
-                    in_=scales_by_run[s, :, units, :],
+                load_given(
+                    s,
+                    d_planes[QUADRANT * s : QUADRANT * s + SCALE_ROWS, columns],
+                    scales_by_run[s, :, units, :],
+                    1,
                 )
-            nc.vector.tensor_copy(
-                out=d_planes[:, columns].bitcast(I32).rearrange("q (o w) -> q o w", w=1),
-                in_=s_landed[:, :, 0:1],
-            )
 
             w_raw = loads.tile([P, I], BF16)
             nc.scalar.dma_start(out=w_raw[:], in_=weight[units, :])
@@ -188,17 +188,14 @@ def tile_advancedneuroplasticitylayer_w_e_kernel(
 
             pre = sums.tile([P, P * SEG], F32)
             for c in range(PASSES):
-                d_landed = given.tile([P, P, BLOCK_WORDS], I32)
+                d_words = given.tile([P, P * SEG], U32, align_bytes=64)
                 for s in range(RUNS):
-                    nc.sync.dma_start(
-                        out=d_landed[QUADRANT * s : QUADRANT * (s + 1), :, 0:SEG],
-                        in_=words_by_run[s, QUADRANT * c : QUADRANT * (c + 1), units, :],
+                    load_given(
+                        s,
+                        d_words[QUADRANT * s : QUADRANT * (s + 1), :],
+                        words_by_run[s, QUADRANT * c : QUADRANT * (c + 1), units, :],
+                        SEG,
                     )
-                d_words = work.tile([P, P * SEG], U32, align_bytes=64)
-                nc.vector.tensor_copy(
-                    out=d_words[:].bitcast(I32).rearrange("r (o j) -> r o j", j=SEG),
-                    in_=d_landed[:, :, 0:SEG],
-                )
                 rows = slice(c * B, (c + 1) * B)
                 nc.tensor.matmul_mx(
                     out=pre[:],

@@ -117,7 +117,7 @@ def tile_advancedneuroplasticitylayer_w_e_kernel(
         scales_by_run = dendrite_segments_scales.rearrange("(o s) q n -> s q o n", s=RUNS)
 
         def load_given(s, sbuf_bytes, hbm_bytes, run_words):
-            queue, word = (nc.sync, I32) if s % 2 == 0 else (nc.scalar, F32)
+            queue, word = (nc.sync, I32) if s < RUNS // 2 else (nc.scalar, F32)
             queue.dma_start(
                 out=sbuf_bytes.bitcast(word).rearrange("r (o w) -> r o w", w=run_words),
                 in_=hbm_bytes.bitcast(word),

@@ -25,6 +25,8 @@ QUADRANT = P // RUNS
 RUN_SHARE = QUADRANT * PACK
 SCALE_ROWS = K_PASS // 32
 O_BLOCKS = O // P
+LOAD_BLOCKS = 2
+LOADS = O_BLOCKS // LOAD_BLOCKS
 PAIRS = PACK // 2
 PASS_PAIRS = K_PASS // 2
 
@@ -50,11 +52,13 @@ def tile_advancedneuroplasticitylayer_w_e_kernel(
             nc.allow_non_contiguous_dma(reason="the given bytes lie in runs of 16 and 4 bytes")
         )
         const = stack.enter_context(tc.tile_pool(name="const", bufs=1))
-        given = stack.enter_context(tc.tile_pool(name="given", bufs=3))
+        given = stack.enter_context(tc.tile_pool(name="given", bufs=2))
         loads = stack.enter_context(tc.tile_pool(name="loads", bufs=3))
         work = stack.enter_context(tc.tile_pool(name="work", bufs=2))
+        kept = stack.enter_context(tc.tile_pool(name="kept", bufs=2 * LOAD_BLOCKS))
         turned = stack.enter_context(tc.psum_pool(name="turned", bufs=2))
         sums = stack.enter_context(tc.psum_pool(name="sums", bufs=2))
+        dendrite_sums = stack.enter_context(tc.psum_pool(name="dendrite_sums", bufs=2 * LOAD_BLOCKS))
 
         ident = const.tile([P, P], F32)
         make_identity(nc, ident[:])
@@ -123,22 +127,8 @@ def tile_advancedneuroplasticitylayer_w_e_kernel(
                 in_=hbm_bytes.bitcast(word),
             )
 
-        d_planes = const.tile([P, O * SEG], U8, align_bytes=64)
-        nc.vector.memset(d_planes[:].bitcast(I32), 0)
-        out_sb = const.tile([P, O], F32)
-
-        for ob in range(O_BLOCKS):
+        def gated_linear(ob):
             units = slice(ob * P, (ob + 1) * P)
-            columns = slice(ob * P * SEG, (ob + 1) * P * SEG)
-
-            for s in range(RUNS):
-                load_given(
-                    s,
-                    d_planes[QUADRANT * s : QUADRANT * s + SCALE_ROWS, columns],
-                    scales_by_run[s, :, units, :],
-                    1,
-                )
-
             w_raw = loads.tile([P, I], BF16)
             nc.scalar.dma_start(out=w_raw[:], in_=weight[units, :])
             wg = work.tile([P, I], BF16)
@@ -183,42 +173,65 @@ def tile_advancedneuroplasticitylayer_w_e_kernel(
                     start=(c == 0),
                     stop=(c == PASSES - 1),
                 )
-            lin_bias = work.tile([P, P], F32)
+            lin_bias = kept.tile([P, P], F32)
             nc.vector.tensor_tensor(out=lin_bias[:], in0=lin[:], in1=bias_all[:, units], op=ALU.add)
 
-            pre = sums.tile([P, P * SEG], F32)
+            return lin_bias
+
+        out_sb = const.tile([P, O], F32)
+
+        for load in range(LOADS):
+            blocks = range(load * LOAD_BLOCKS, (load + 1) * LOAD_BLOCKS)
+            load_units = slice(load * LOAD_BLOCKS * P, (load + 1) * LOAD_BLOCKS * P)
+
+            d_planes = given.tile([P, LOAD_BLOCKS * P * SEG], U8, align_bytes=64)
+            nc.vector.memset(d_planes[:].bitcast(I32), 0)
+            for s in range(RUNS):
+                load_given(
+                    s,
+                    d_planes[QUADRANT * s : QUADRANT * s + SCALE_ROWS, :],
+                    scales_by_run[s, :, load_units, :],
+                    1,
+                )
+
+            lin_biases = [gated_linear(ob) for ob in blocks]
+
+            pres = [dendrite_sums.tile([P, P * SEG], F32, name="pre") for ob in blocks]
             for c in range(PASSES):
-                d_words = given.tile([P, P * SEG], U32, align_bytes=64)
+                d_words = given.tile([P, LOAD_BLOCKS * P * SEG], U32, align_bytes=64)
                 for s in range(RUNS):
                     load_given(
                         s,
                         d_words[QUADRANT * s : QUADRANT * (s + 1), :],
-                        words_by_run[s, QUADRANT * c : QUADRANT * (c + 1), units, :],
+                        words_by_run[s, QUADRANT * c : QUADRANT * (c + 1), load_units, :],
                         SEG,
                     )
                 rows = slice(c * B, (c + 1) * B)
-                nc.tensor.matmul_mx(
-                    out=pre[:],
-                    lhsT=x_words[:, rows].bitcast(FP8X4),
-                    lhsT_scale=x_planes[:, rows],
-                    rhs=d_words[:].bitcast(FP8X4),
-                    rhs_scale=d_planes[4 * c : P, columns],
-                    start=(c == 0),
-                    stop=(c == PASSES - 1),
-                )
+                for h, ob in enumerate(blocks):
+                    nc.tensor.matmul_mx(
+                        out=pres[h][:],
+                        lhsT=x_words[:, rows].bitcast(FP8X4),
+                        lhsT_scale=x_planes[:, rows],
+                        rhs=d_words[:, h * P * SEG : (h + 1) * P * SEG].bitcast(FP8X4),
+                        rhs_scale=d_planes[4 * c : P, h * P * SEG : (h + 1) * P * SEG],
+                        start=(c == 0),
+                        stop=(c == PASSES - 1),
+                    )
 
-            relu = work.tile([P, P * SEG], F32)
-            nc.scalar.activation(out=relu[:], in_=pre[:], func=ACT.Relu)
-            dendritic = work.tile([P, P], F32)
-            nc.vector.tensor_reduce(
-                out=dendritic[:],
-                in_=relu[:].rearrange("p (o j) -> p o j", j=SEG),
-                axis=mybir.AxisListType.X,
-                op=ALU.add,
-            )
-            nc.vector.tensor_tensor(
-                out=out_sb[:, units], in0=lin_bias[:], in1=dendritic[:], op=ALU.add
-            )
-            if ob % 4 == 3:
-                done = slice((ob - 3) * P, (ob + 1) * P)
+            for h, ob in enumerate(blocks):
+                units = slice(ob * P, (ob + 1) * P)
+                relu = work.tile([P, P * SEG], F32)
+                nc.scalar.activation(out=relu[:], in_=pres[h][:], func=ACT.Relu)
+                dendritic = work.tile([P, P], F32)
+                nc.vector.tensor_reduce(
+                    out=dendritic[:],
+                    in_=relu[:].rearrange("p (o j) -> p o j", j=SEG),
+                    axis=mybir.AxisListType.X,
+                    op=ALU.add,
+                )
+                nc.vector.tensor_tensor(
+                    out=out_sb[:, units], in0=lin_biases[h][:], in1=dendritic[:], op=ALU.add
+                )
+            if load % 2 == 1:
+                done = slice((load - 1) * LOAD_BLOCKS * P, (load + 1) * LOAD_BLOCKS * P)
                 nc.scalar.dma_start(out=out[:, done], in_=out_sb[:, done])

@@ -94,25 +94,21 @@ def tile_advancedneuroplasticitylayer_w_e_kernel(
             in_=x_grouped[:].rearrange("p c b t -> p (c b t)"),
         )
 
-        vectors = const.tile([P, 2, P], BF16)
-        nc.vector.memset(vectors[:], 0.0)
+        vectors = const.tile([P, 2, O_BLOCKS], BF16)
         nc.scalar.dma_start(
-            out=vectors[0:O_BLOCKS, 0, :],
-            in_=astrocyte_activation.rearrange("(r c) -> r c", c=P),
+            out=vectors[:, 0, :].rearrange("p (h l) -> p h l", l=LOADS),
+            in_=astrocyte_activation.rearrange("(h p l) -> p h l", p=P, l=LOADS),
         )
         nc.scalar.dma_start(
-            out=vectors[0:O_BLOCKS, 1, :], in_=context.rearrange("(r c) -> r c", c=P)
+            out=vectors[:, 1, :].rearrange("p (h l) -> p h l", l=LOADS),
+            in_=context.rearrange("(h p l) -> p h l", p=P, l=LOADS),
         )
-        product = const.tile([P, P], F32)
+        product = const.tile([P, O_BLOCKS], F32)
         nc.vector.tensor_tensor(
             out=product[:], in0=vectors[:, 0, :], in1=vectors[:, 1, :], op=ALU.mult
         )
-        gate_rows = const.tile([P, P], F32)
-        nc.scalar.activation(out=gate_rows[:], in_=product[:], func=ACT.Sigmoid)
-        gate_ps = turned.tile([P, P], F32, tag="w_ps")
-        nc.tensor.transpose(gate_ps[:], gate_rows[:], ident[:])
         gate = const.tile([P, O_BLOCKS], F32)
-        nc.vector.tensor_copy(out=gate[:], in_=gate_ps[:, 0:O_BLOCKS])
+        nc.scalar.activation(out=gate[:], in_=product[:], func=ACT.Sigmoid)
 
         bias_all = const.tile([P, O], BF16)
         nc.scalar.dma_start(out=bias_all[:], in_=bias.partition_broadcast(P))
@@ -127,15 +123,18 @@ def tile_advancedneuroplasticitylayer_w_e_kernel(
                 in_=hbm_bytes.bitcast(word),
             )
 
-        def gated_linear(ob):
-            units = slice(ob * P, (ob + 1) * P)
+        def block_units(load, h):
+            return slice(LOADS * P * h + load, LOADS * P * (h + 1), LOADS)
+
+        def gated_linear(load, h):
+            units = block_units(load, h)
             w_raw = loads.tile([P, I], BF16)
             nc.scalar.dma_start(out=w_raw[:], in_=weight[units, :])
             wg = work.tile([P, I], BF16)
             nc.vector.tensor_scalar_mul(
                 out=wg[:].rearrange("o (c s e) -> o c s e", c=PASSES, s=RUNS),
                 in0=w_raw[:].rearrange("o (s c e) -> o c s e", c=PASSES, s=RUNS),
-                scalar1=gate[:, ob : ob + 1],
+                scalar1=gate[:, LOADS * h + load : LOADS * h + load + 1],
             )
             w_grouped = work.tile([P, PASSES, P, PACK], BF16, align_bytes=64)
             for half in range(2):
@@ -181,8 +180,8 @@ def tile_advancedneuroplasticitylayer_w_e_kernel(
         out_sb = const.tile([P, O], F32)
 
         for load in range(LOADS):
-            blocks = range(load * LOAD_BLOCKS, (load + 1) * LOAD_BLOCKS)
-            load_units = slice(load * LOAD_BLOCKS * P, (load + 1) * LOAD_BLOCKS * P)
+            blocks = range(LOAD_BLOCKS)
+            load_units = slice(load, O, LOADS)
 
             d_planes = given.tile([P, LOAD_BLOCKS * P * SEG], U8, align_bytes=64)
             nc.vector.memset(d_planes[:].bitcast(I32), 0)
@@ -194,9 +193,9 @@ def tile_advancedneuroplasticitylayer_w_e_kernel(
                     1,
                 )
 
-            lin_biases = [gated_linear(ob) for ob in blocks]
+            lin_biases = [gated_linear(load, h) for h in blocks]
 
-            pres = [dendrite_sums.tile([P, P * SEG], F32, name="pre") for ob in blocks]
+            pres = [dendrite_sums.tile([P, P * SEG], F32, name="pre") for h in blocks]
             for c in range(PASSES):
                 d_words = given.tile([P, LOAD_BLOCKS * P * SEG], U32, align_bytes=64)
                 for s in range(RUNS):
@@ -207,7 +206,7 @@ def tile_advancedneuroplasticitylayer_w_e_kernel(
                         SEG,
                     )
                 rows = slice(c * B, (c + 1) * B)
-                for h, ob in enumerate(blocks):
+                for h in blocks:
                     nc.tensor.matmul_mx(
                         out=pres[h][:],
                         lhsT=x_words[:, rows].bitcast(FP8X4),
@@ -218,8 +217,8 @@ def tile_advancedneuroplasticitylayer_w_e_kernel(
                         stop=(c == PASSES - 1),
                     )
 
-            for h, ob in enumerate(blocks):
-                units = slice(ob * P, (ob + 1) * P)
+            for h in blocks:
+                units = block_units(load, h)
                 relu = work.tile([P, P * SEG], F32)
                 nc.scalar.activation(out=relu[:], in_=pres[h][:], func=ACT.Relu)
                 dendritic = work.tile([P, P], F32)
@@ -232,6 +231,5 @@ def tile_advancedneuroplasticitylayer_w_e_kernel(
                 nc.vector.tensor_tensor(
                     out=out_sb[:, units], in0=lin_biases[h][:], in1=dendritic[:], op=ALU.add
                 )
-            if load % 2 == 1:
-                done = slice((load - 1) * LOAD_BLOCKS * P, (load + 1) * LOAD_BLOCKS * P)
-                nc.scalar.dma_start(out=out[:, done], in_=out_sb[:, done])
+
+        nc.sync.dma_start(out=out, in_=out_sb[:])

@@ -94,21 +94,25 @@ def tile_advancedneuroplasticitylayer_w_e_kernel(
             in_=x_grouped[:].rearrange("p c b t -> p (c b t)"),
         )
 
-        vectors = const.tile([P, 2, O_BLOCKS], BF16)
+        vectors = const.tile([P, 2, P], BF16)
+        nc.vector.memset(vectors[:], 0.0)
         nc.scalar.dma_start(
-            out=vectors[:, 0, :].rearrange("p (h l) -> p h l", l=LOADS),
-            in_=astrocyte_activation.rearrange("(h p l) -> p h l", p=P, l=LOADS),
+            out=vectors[0:O_BLOCKS, 0, :],
+            in_=astrocyte_activation.rearrange("(r c) -> r c", c=P),
         )
         nc.scalar.dma_start(
-            out=vectors[:, 1, :].rearrange("p (h l) -> p h l", l=LOADS),
-            in_=context.rearrange("(h p l) -> p h l", p=P, l=LOADS),
+            out=vectors[0:O_BLOCKS, 1, :], in_=context.rearrange("(r c) -> r c", c=P)
         )
-        product = const.tile([P, O_BLOCKS], F32)
+        product = const.tile([P, P], F32)
         nc.vector.tensor_tensor(
             out=product[:], in0=vectors[:, 0, :], in1=vectors[:, 1, :], op=ALU.mult
         )
+        gate_rows = const.tile([P, P], F32)
+        nc.scalar.activation(out=gate_rows[:], in_=product[:], func=ACT.Sigmoid)
+        gate_ps = turned.tile([P, P], F32, tag="w_ps")
+        nc.tensor.transpose(gate_ps[:], gate_rows[:], ident[:])
         gate = const.tile([P, O_BLOCKS], F32)
-        nc.scalar.activation(out=gate[:], in_=product[:], func=ACT.Sigmoid)
+        nc.vector.tensor_copy(out=gate[:], in_=gate_ps[:, 0:O_BLOCKS])
 
         bias_all = const.tile([P, O], BF16)
         nc.scalar.dma_start(out=bias_all[:], in_=bias.partition_broadcast(P))
@@ -117,24 +121,26 @@ def tile_advancedneuroplasticitylayer_w_e_kernel(
         scales_by_run = dendrite_segments_scales.rearrange("(o s) q n -> s q o n", s=RUNS)
 
         def load_given(s, sbuf_bytes, hbm_bytes, run_words):
-            queue, word = (nc.sync, I32) if s < RUNS // 2 else (nc.scalar, F32)
+            if s >= RUNS // 2:
+                queue, word = nc.gpsimd, F32
+            elif s == 1:
+                queue, word = nc.scalar, F32
+            else:
+                queue, word = nc.sync, I32
             queue.dma_start(
                 out=sbuf_bytes.bitcast(word).rearrange("r (o w) -> r o w", w=run_words),
                 in_=hbm_bytes.bitcast(word),
             )
 
-        def block_units(load, h):
-            return slice(LOADS * P * h + load, LOADS * P * (h + 1), LOADS)
-
-        def gated_linear(load, h):
-            units = block_units(load, h)
+        def gated_linear(ob):
+            units = slice(ob * P, (ob + 1) * P)
             w_raw = loads.tile([P, I], BF16)
             nc.scalar.dma_start(out=w_raw[:], in_=weight[units, :])
             wg = work.tile([P, I], BF16)
             nc.vector.tensor_scalar_mul(
                 out=wg[:].rearrange("o (c s e) -> o c s e", c=PASSES, s=RUNS),
                 in0=w_raw[:].rearrange("o (s c e) -> o c s e", c=PASSES, s=RUNS),
-                scalar1=gate[:, LOADS * h + load : LOADS * h + load + 1],
+                scalar1=gate[:, ob : ob + 1],
             )
             w_grouped = work.tile([P, PASSES, P, PACK], BF16, align_bytes=64)
             for half in range(2):
@@ -180,8 +186,8 @@ def tile_advancedneuroplasticitylayer_w_e_kernel(
         out_sb = const.tile([P, O], F32)
 
         for load in range(LOADS):
-            blocks = range(LOAD_BLOCKS)
-            load_units = slice(load, O, LOADS)
+            blocks = range(load * LOAD_BLOCKS, (load + 1) * LOAD_BLOCKS)
+            load_units = slice(load * LOAD_BLOCKS * P, (load + 1) * LOAD_BLOCKS * P)
 
             d_planes = given.tile([P, LOAD_BLOCKS * P * SEG], U8, align_bytes=64)
             nc.vector.memset(d_planes[:].bitcast(I32), 0)
@@ -193,9 +199,9 @@ def tile_advancedneuroplasticitylayer_w_e_kernel(
                     1,
                 )
 
-            lin_biases = [gated_linear(load, h) for h in blocks]
+            lin_biases = [gated_linear(ob) for ob in blocks]
 
-            pres = [dendrite_sums.tile([P, P * SEG], F32, name="pre") for h in blocks]
+            pres = [dendrite_sums.tile([P, P * SEG], F32, name="pre") for ob in blocks]
             for c in range(PASSES):
                 d_words = given.tile([P, LOAD_BLOCKS * P * SEG], U32, align_bytes=64)
                 for s in range(RUNS):
@@ -206,7 +212,7 @@ def tile_advancedneuroplasticitylayer_w_e_kernel(
                         SEG,
                     )
                 rows = slice(c * B, (c + 1) * B)
-                for h in blocks:
+                for h, ob in enumerate(blocks):
                     nc.tensor.matmul_mx(
                         out=pres[h][:],
                         lhsT=x_words[:, rows].bitcast(FP8X4),
@@ -217,8 +223,8 @@ def tile_advancedneuroplasticitylayer_w_e_kernel(
                         stop=(c == PASSES - 1),
                     )
 
-            for h in blocks:
-                units = block_units(load, h)
+            for h, ob in enumerate(blocks):
+                units = slice(ob * P, (ob + 1) * P)
                 relu = work.tile([P, P * SEG], F32)
                 nc.scalar.activation(out=relu[:], in_=pres[h][:], func=ACT.Relu)
                 dendritic = work.tile([P, P], F32)
@@ -231,5 +237,6 @@ def tile_advancedneuroplasticitylayer_w_e_kernel(
                 nc.vector.tensor_tensor(
                     out=out_sb[:, units], in0=lin_biases[h][:], in1=dendritic[:], op=ALU.add
                 )
-
-        nc.sync.dma_start(out=out, in_=out_sb[:])
+            if load % 2 == 1:
+                done = slice((load - 1) * LOAD_BLOCKS * P, (load + 1) * LOAD_BLOCKS * P)
+                nc.scalar.dma_start(out=out[:, done], in_=out_sb[:, done])

@@ -121,9 +121,9 @@ def tile_advancedneuroplasticitylayer_w_e_kernel(
         scales_by_run = dendrite_segments_scales.rearrange("(o s) q n -> s q o n", s=RUNS)
 
         def load_given(s, sbuf_bytes, hbm_bytes, run_words):
-            if s >= RUNS // 2:
+            if s == RUNS - 1:
                 queue, word = nc.gpsimd, F32
-            elif s == 1:
+            elif s % 2 == 1:
                 queue, word = nc.scalar, F32
             else:
                 queue, word = nc.sync, I32

from contextlib import ExitStack

import concourse.mybir as mybir
from concourse.masks import make_identity

F32 = mybir.dt.float32
BF16 = mybir.dt.bfloat16
I32 = mybir.dt.int32
U32 = mybir.dt.uint32
U8 = mybir.dt.uint8
FP8X4 = mybir.dt.float8_e4m3fn_x4
ALU = mybir.AluOpType
ACT = mybir.ActivationFunctionType

P = 128
B = 128
I = 2048
O = 2048
SEG = 4
PACK = 4
K_PASS = P * PACK
PASSES = I // K_PASS
RUNS = I // K_PASS
QUADRANT = P // RUNS
RUN_SHARE = QUADRANT * PACK
SCALE_ROWS = K_PASS // 32
O_BLOCKS = O // P
LOAD_BLOCKS = 2
LOADS = O_BLOCKS // LOAD_BLOCKS
PAIRS = PACK // 2
PASS_PAIRS = K_PASS // 2

FLOPS = 2 * B * I * (O * SEG + O)
BYTES = 2 * (B * I + O * I + 3 * O) + O * I * SEG + O * I * SEG // 32 + 4 * B * O


def tile_advancedneuroplasticitylayer_w_e_kernel(
    tc,
    x,
    context,
    prev_activation,
    weight,
    bias,
    astrocyte_activation,
    dendrite_segments_words,
    dendrite_segments_scales,
    out,
):
    nc = tc.nc
    with ExitStack() as stack:
        stack.enter_context(
            nc.allow_non_contiguous_dma(reason="the given bytes lie in runs of 16 and 4 bytes")
        )
        const = stack.enter_context(tc.tile_pool(name="const", bufs=1))
        given = stack.enter_context(tc.tile_pool(name="given", bufs=2))
        loads = stack.enter_context(tc.tile_pool(name="loads", bufs=3))
        work = stack.enter_context(tc.tile_pool(name="work", bufs=2))
        kept = stack.enter_context(tc.tile_pool(name="kept", bufs=2 * LOAD_BLOCKS))
        turned = stack.enter_context(tc.psum_pool(name="turned", bufs=2))
        sums = stack.enter_context(tc.psum_pool(name="sums", bufs=2))
        dendrite_sums = stack.enter_context(tc.psum_pool(name="dendrite_sums", bufs=2 * LOAD_BLOCKS))

        ident = const.tile([P, P], F32)
        make_identity(nc, ident[:])

        x_sb = const.tile([P, I], BF16)
        nc.scalar.dma_start(out=x_sb[:], in_=x)
        x_sorted = const.tile([P, I], BF16)
        nc.vector.tensor_copy(
            out=x_sorted[:].rearrange("b (c s e) -> b c s e", c=PASSES, s=RUNS),
            in_=x_sb[:].rearrange("b (s c e) -> b c s e", c=PASSES, s=RUNS),
        )
        x_pairs = x_sorted[:].bitcast(F32)
        x_grouped = const.tile([P, PASSES, B, PACK], BF16, align_bytes=64)
        for half in range(2):
            x_ps = turned.tile([P, 2, PAIRS, B], F32, tag="w_ps")
            for ci in range(2):
                c = 2 * half + ci
                for u in range(PAIRS):
                    nc.tensor.transpose(
                        x_ps[:, ci, u, :],
                        x_pairs[:, PASS_PAIRS * c + u : PASS_PAIRS * (c + 1) : PAIRS],
                        ident[:],
                    )
            nc.vector.tensor_copy(
                out=x_grouped[:, 2 * half : 2 * half + 2].bitcast(F32),
                in_=x_ps[:].rearrange("p c u b -> p c b u"),
            )
        x_words = const.tile([P, PASSES * B], U32, align_bytes=64)
        x_planes = const.tile([P, PASSES * B], U8, align_bytes=64)
        nc.vector.quantize_mx(
            out=x_words[:].bitcast(FP8X4),
            scales=x_planes[:],
            in_=x_grouped[:].rearrange("p c b t -> p (c b t)"),
        )

        vectors = const.tile([P, 2, P], BF16)
        nc.vector.memset(vectors[:], 0.0)
        nc.scalar.dma_start(
            out=vectors[0:O_BLOCKS, 0, :],
            in_=astrocyte_activation.rearrange("(r c) -> r c", c=P),
        )
        nc.scalar.dma_start(
            out=vectors[0:O_BLOCKS, 1, :], in_=context.rearrange("(r c) -> r c", c=P)
        )
        product = const.tile([P, P], F32)
        nc.vector.tensor_tensor(
            out=product[:], in0=vectors[:, 0, :], in1=vectors[:, 1, :], op=ALU.mult
        )
        gate_rows = const.tile([P, P], F32)
        nc.scalar.activation(out=gate_rows[:], in_=product[:], func=ACT.Sigmoid)
        gate_ps = turned.tile([P, P], F32, tag="w_ps")
        nc.tensor.transpose(gate_ps[:], gate_rows[:], ident[:])
        gate = const.tile([P, O_BLOCKS], F32)
        nc.vector.tensor_copy(out=gate[:], in_=gate_ps[:, 0:O_BLOCKS])

        bias_all = const.tile([P, O], BF16)
        nc.scalar.dma_start(out=bias_all[:], in_=bias.partition_broadcast(P))

        words_by_run = dendrite_segments_words.rearrange("(o s) p n t -> s p o (n t)", s=RUNS)
        scales_by_run = dendrite_segments_scales.rearrange("(o s) q n -> s q o n", s=RUNS)

        def load_given(s, sbuf_bytes, hbm_bytes, run_words):
            if s == RUNS - 1:
                queue, word = nc.gpsimd, F32
            elif s % 2 == 1:
                queue, word = nc.scalar, F32
            else:
                queue, word = nc.sync, I32
            queue.dma_start(
                out=sbuf_bytes.bitcast(word).rearrange("r (o w) -> r o w", w=run_words),
                in_=hbm_bytes.bitcast(word),
            )

        def gated_linear(ob):
            units = slice(ob * P, (ob + 1) * P)
            w_raw = loads.tile([P, I], BF16)
            nc.scalar.dma_start(out=w_raw[:], in_=weight[units, :])
            wg = work.tile([P, I], BF16)
            nc.vector.tensor_scalar_mul(
                out=wg[:].rearrange("o (c s e) -> o c s e", c=PASSES, s=RUNS),
                in0=w_raw[:].rearrange("o (s c e) -> o c s e", c=PASSES, s=RUNS),
                scalar1=gate[:, ob : ob + 1],
            )
            w_grouped = work.tile([P, PASSES, P, PACK], BF16, align_bytes=64)
            for half in range(2):
                w_ps = turned.tile([P, 2, PAIRS, P], F32, tag="w_ps")
                for ci in range(2):
                    c = 2 * half + ci
                    for u in range(PAIRS):
                        nc.tensor.transpose(
                            w_ps[:, ci, u, :],
                            wg[:].bitcast(F32)[
                                :, PASS_PAIRS * c + u : PASS_PAIRS * (c + 1) : PAIRS
                            ],
                            ident[:],
                        )
                nc.scalar.copy(
                    out=w_grouped[:, 2 * half : 2 * half + 2].bitcast(F32),
                    in_=w_ps[:].rearrange("p c u o -> p c o u"),
                )
            w_words = work.tile([P, PASSES * P], U32, align_bytes=64)
            w_planes = work.tile([P, PASSES * P], U8, align_bytes=64)
            nc.vector.quantize_mx(
                out=w_words[:].bitcast(FP8X4),
                scales=w_planes[:],
                in_=w_grouped[:].rearrange("p c o t -> p (c o t)"),
            )
            lin = sums.tile([P, P], F32)
            for c in range(PASSES):
                rows = slice(c * B, (c + 1) * B)
                nc.tensor.matmul_mx(
                    out=lin[:],
                    lhsT=x_words[:, rows].bitcast(FP8X4),
                    lhsT_scale=x_planes[:, rows],
                    rhs=w_words[:, c * P : (c + 1) * P].bitcast(FP8X4),
                    rhs_scale=w_planes[:, c * P : (c + 1) * P],
                    start=(c == 0),
                    stop=(c == PASSES - 1),
                )
            lin_bias = kept.tile([P, P], F32)
            nc.vector.tensor_tensor(out=lin_bias[:], in0=lin[:], in1=bias_all[:, units], op=ALU.add)

            return lin_bias

        out_sb = const.tile([P, O], F32)

        for load in range(LOADS):
            blocks = range(load * LOAD_BLOCKS, (load + 1) * LOAD_BLOCKS)
            load_units = slice(load * LOAD_BLOCKS * P, (load + 1) * LOAD_BLOCKS * P)

            d_planes = given.tile([P, LOAD_BLOCKS * P * SEG], U8, align_bytes=64)
            nc.vector.memset(d_planes[:].bitcast(I32), 0)
            for s in range(RUNS):
                load_given(
                    s,
                    d_planes[QUADRANT * s : QUADRANT * s + SCALE_ROWS, :],
                    scales_by_run[s, :, load_units, :],
                    1,
                )

            lin_biases = [gated_linear(ob) for ob in blocks]

            pres = [dendrite_sums.tile([P, P * SEG], F32, name="pre") for ob in blocks]
            for c in range(PASSES):
                d_words = given.tile([P, LOAD_BLOCKS * P * SEG], U32, align_bytes=64)
                for s in range(RUNS):
                    load_given(
                        s,
                        d_words[QUADRANT * s : QUADRANT * (s + 1), :],
                        words_by_run[s, QUADRANT * c : QUADRANT * (c + 1), load_units, :],
                        SEG,
                    )
                rows = slice(c * B, (c + 1) * B)
                for h, ob in enumerate(blocks):
                    nc.tensor.matmul_mx(
                        out=pres[h][:],
                        lhsT=x_words[:, rows].bitcast(FP8X4),
                        lhsT_scale=x_planes[:, rows],
                        rhs=d_words[:, h * P * SEG : (h + 1) * P * SEG].bitcast(FP8X4),
                        rhs_scale=d_planes[4 * c : P, h * P * SEG : (h + 1) * P * SEG],
                        start=(c == 0),
                        stop=(c == PASSES - 1),
                    )

            for h, ob in enumerate(blocks):
                units = slice(ob * P, (ob + 1) * P)
                relu = work.tile([P, P * SEG], F32)
                nc.scalar.activation(out=relu[:], in_=pres[h][:], func=ACT.Relu)
                dendritic = work.tile([P, P], F32)
                nc.vector.tensor_reduce(
                    out=dendritic[:],
                    in_=relu[:].rearrange("p (o j) -> p o j", j=SEG),
                    axis=mybir.AxisListType.X,
                    op=ALU.add,
                )
                nc.vector.tensor_tensor(
                    out=out_sb[:, units], in0=lin_biases[h][:], in1=dendritic[:], op=ALU.add
                )
            if load % 2 == 1:
                done = slice((load - 1) * LOAD_BLOCKS * P, (load + 1) * LOAD_BLOCKS * P)
                nc.scalar.dma_start(out=out[:, done], in_=out_sb[:, done])
